import numpy as np
import ml_dtypes

BF16 = ml_dtypes.bfloat16


def bf(x):
    return np.asarray(x, np.float32).astype(BF16)


def f32(x):
    return np.asarray(x, np.float32)


def f64(x):
    return np.asarray(x).astype(np.float64)


def striped(idx):
    return np.tile(idx.reshape(-1, 16).T, (8, 1))


C, R, N, S = 256, 256, 128, 512


def setup_inputs():
    return {"feat": bf(np.random.standard_normal((C, R))), "w": bf(np.random.standard_normal((C, N)) / np.sqrt(C)), "base": f32(0.15 * np.random.standard_normal((C, S))), "offs": striped(np.random.permutation(S)[:N])}


def reference(feat, w, base, offs):
    idx = offs[:16].T.reshape(-1)
    x = f64(feat)
    e = np.exp(x.T @ f64(w))
    a = e / e.sum(axis=1, keepdims=True)
    size = a.sum(axis=0, keepdims=True)
    out = f64(base).copy()
    out[:, idx] = (x @ a) * (1.0 / size)
    return out

@@ -1,0 +1,92 @@
+import concourse.mybir as mybir
+from concourse.masks import make_identity
+
+P = 128
+C, R, N, S = 256, 256, 128, 512
+CB = C // P
+RB = R // P
+
+FLOPS = 2 * R * C * N + 2 * C * R * N + 2 * R * N
+
+BF16, F32, U16 = mybir.dt.bfloat16, mybir.dt.float32, mybir.dt.uint16
+EXP = mybir.ActivationFunctionType.Exp
+MULT, MAX = mybir.AluOpType.mult, mybir.AluOpType.max
+X = mybir.AxisListType.X
+
+
+def tile_diffpooling_kernel(tc, feat, w, base, offs, out):
+    nc = tc.nc
+    with (
+        tc.tile_pool(name="held", bufs=1) as held,
+        tc.psum_pool(name="psum", bufs=1) as psum,
+    ):
+        feat_sb = held.tile([P, CB, R], BF16, name="feat_sb")
+        w_sb = held.tile([P, CB, N], BF16, name="w_sb")
+        offsets = held.tile([P, N // 16], U16, name="offsets")
+        windows = [held.tile([P, S], F32, name=f"window{cb}") for cb in range(CB)]
+        nc.sync.dma_start(feat_sb[:], feat.rearrange("(b p) r -> p b r", p=P))
+        nc.scalar.dma_start(w_sb[:], w.rearrange("(b p) i -> p b i", p=P))
+        nc.sync.dma_start(offsets[:], offs)
+        for cb in range(CB):
+            nc.sync.dma_start(windows[cb][:], base[cb * P : (cb + 1) * P, :])
+
+        identity = held.tile([P, P], BF16, name="identity")
+        make_identity(nc, identity[:])
+        ones = held.tile([P, P], BF16, name="ones")
+        nc.gpsimd.memset(ones[:], 1.0)
+
+        t_ps = [psum.tile([P, N], F32, name=f"t_ps{rb}") for rb in range(RB)]
+        for rb in range(RB):
+            for cb in range(CB):
+                nc.tensor.matmul(
+                    t_ps[rb][:],
+                    feat_sb[:, cb, rb * P : (rb + 1) * P],
+                    w_sb[:, cb, :],
+                    start=(cb == 0),
+                    stop=(cb == CB - 1),
+                )
+
+        featT_ps = psum.tile([P, RB, C], BF16, name="featT_ps")
+        for rb in range(RB):
+            for cb in range(CB):
+                nc.tensor.transpose(
+                    featT_ps[:, rb, cb * P : (cb + 1) * P],
+                    feat_sb[:, cb, rb * P : (rb + 1) * P],
+                    identity[:],
+                )
+        featT_sb = held.tile([P, RB, C], BF16, name="featT_sb")
+        nc.vector.tensor_copy(featT_sb[:], featT_ps[:])
+
+        a_sb = held.tile([P, RB, N], BF16, name="a_sb")
+        for rb in range(RB):
+            neg_max = held.tile([P, 1], F32, name=f"neg_max{rb}")
+            nc.vector.tensor_reduce(neg_max[:], t_ps[rb][:], axis=X, op=MAX, negate=True)
+            e_sb = held.tile([P, N], F32, name=f"e_sb{rb}")
+            e_sum = held.tile([P, 1], F32, name=f"e_sum{rb}")
+            nc.scalar.activation(e_sb[:], t_ps[rb][:], EXP, bias=neg_max[:], accum_out=e_sum[:])
+            e_rsum = held.tile([P, 1], F32, name=f"e_rsum{rb}")
+            nc.vector.reciprocal(e_rsum[:], e_sum[:])
+            nc.vector.tensor_scalar(a_sb[:, rb, :], e_sb[:], e_rsum[:], None, op0=MULT)
+
+        size_ps = psum.tile([P, N], F32, name="size_ps")
+        for rb in range(RB):
+            nc.tensor.matmul(
+                size_ps[:], ones[:], a_sb[:, rb, :], start=(rb == 0), stop=(rb == RB - 1)
+            )
+        rsize = held.tile([P, N], F32, name="rsize")
+        nc.vector.reciprocal(rsize[:], size_ps[:])
+
+        for cb in range(CB):
+            u_ps = psum.tile([P, N], F32, name=f"u_ps{cb}")
+            for rb in range(RB):
+                nc.tensor.matmul(
+                    u_ps[:],
+                    featT_sb[:, rb, cb * P : (cb + 1) * P],
+                    a_sb[:, rb, :],
+                    start=(rb == 0),
+                    stop=(rb == RB - 1),
+                )
+            u_sb = held.tile([P, N], F32, name=f"u_sb{cb}")
+            nc.scalar.copy(u_sb[:], u_ps[:])
+            nc.vector.tensor_tensor(windows[cb][:].indirect(offsets[:]), u_sb[:], rsize[:], MULT)
+            nc.sync.dma_start(out[cb * P : (cb + 1) * P, :], windows[cb][:])

@@ -46,32 +46,36 @@ def tile_diffpooling_kernel(tc, feat, w, base, offs, out):
                     stop=(cb == CB - 1),
                 )
 
-        featT_ps = psum.tile([P, RB, C], BF16, name="featT_ps")
+        featT_ps = [psum.tile([P, C], BF16, name=f"featT_ps{rb}") for rb in range(RB)]
         for rb in range(RB):
             for cb in range(CB):
                 nc.tensor.transpose(
-                    featT_ps[:, rb, cb * P : (cb + 1) * P],
+                    featT_ps[rb][:, cb * P : (cb + 1) * P],
                     feat_sb[:, cb, rb * P : (rb + 1) * P],
                     identity[:],
                 )
-        featT_sb = held.tile([P, RB, C], BF16, name="featT_sb")
-        nc.vector.tensor_copy(featT_sb[:], featT_ps[:])
+        featT_sb = [held.tile([P, C], BF16, name=f"featT_sb{rb}") for rb in range(RB)]
 
-        a_sb = held.tile([P, RB, N], BF16, name="a_sb")
+        neg_max = [held.tile([P, 1], F32, name=f"neg_max{rb}") for rb in range(RB)]
+        e_sb = [held.tile([P, N], F32, name=f"e_sb{rb}") for rb in range(RB)]
+        e_sum = [held.tile([P, 1], F32, name=f"e_sum{rb}") for rb in range(RB)]
+        e_rsum = [held.tile([P, 1], F32, name=f"e_rsum{rb}") for rb in range(RB)]
+        a_sb = [held.tile([P, N], BF16, name=f"a_sb{rb}") for rb in range(RB)]
         for rb in range(RB):
-            neg_max = held.tile([P, 1], F32, name=f"neg_max{rb}")
-            nc.vector.tensor_reduce(neg_max[:], t_ps[rb][:], axis=X, op=MAX, negate=True)
-            e_sb = held.tile([P, N], F32, name=f"e_sb{rb}")
-            e_sum = held.tile([P, 1], F32, name=f"e_sum{rb}")
-            nc.scalar.activation(e_sb[:], t_ps[rb][:], EXP, bias=neg_max[:], accum_out=e_sum[:])
-            e_rsum = held.tile([P, 1], F32, name=f"e_rsum{rb}")
-            nc.vector.reciprocal(e_rsum[:], e_sum[:])
-            nc.vector.tensor_scalar(a_sb[:, rb, :], e_sb[:], e_rsum[:], None, op0=MULT)
+            nc.vector.tensor_reduce(neg_max[rb][:], t_ps[rb][:], axis=X, op=MAX, negate=True)
+            nc.scalar.activation(
+                e_sb[rb][:], t_ps[rb][:], EXP, bias=neg_max[rb][:], accum_out=e_sum[rb][:]
+            )
+        nc.vector.tensor_copy(featT_sb[0][:], featT_ps[0][:])
+        nc.scalar.copy(featT_sb[1][:], featT_ps[1][:])
+        for rb in range(RB):
+            nc.vector.reciprocal(e_rsum[rb][:], e_sum[rb][:])
+            nc.vector.tensor_scalar(a_sb[rb][:], e_sb[rb][:], e_rsum[rb][:], None, op0=MULT)
 
         size_ps = psum.tile([P, N], F32, name="size_ps")
         for rb in range(RB):
             nc.tensor.matmul(
-                size_ps[:], ones[:], a_sb[:, rb, :], start=(rb == 0), stop=(rb == RB - 1)
+                size_ps[:], ones[:], a_sb[rb][:], start=(rb == 0), stop=(rb == RB - 1)
             )
         rsize = held.tile([P, N], F32, name="rsize")
         nc.vector.reciprocal(rsize[:], size_ps[:])
@@ -81,8 +85,8 @@ def tile_diffpooling_kernel(tc, feat, w, base, offs, out):
             for rb in range(RB):
                 nc.tensor.matmul(
                     u_ps[:],
-                    featT_sb[:, rb, cb * P : (cb + 1) * P],
-                    a_sb[:, rb, :],
+                    featT_sb[rb][:, cb * P : (cb + 1) * P],
+                    a_sb[rb][:],
                     start=(rb == 0),
                     stop=(rb == RB - 1),
                 )

@@ -22,13 +22,15 @@ def tile_diffpooling_kernel(tc, feat, w, base, offs, out):
     ):
         feat_sb = held.tile([P, CB, R], BF16, name="feat_sb")
         w_sb = held.tile([P, CB, N], BF16, name="w_sb")
+        base_blocks = base.rearrange("(p b) s -> p b s", b=CB)
+        out_blocks = out.rearrange("(p b) s -> p b s", b=CB)
         offsets = held.tile([P, N // 16], U16, name="offsets")
         windows = [held.tile([P, S], F32, name=f"window{cb}") for cb in range(CB)]
-        nc.sync.dma_start(feat_sb[:], feat.rearrange("(b p) r -> p b r", p=P))
-        nc.scalar.dma_start(w_sb[:], w.rearrange("(b p) i -> p b i", p=P))
+        nc.sync.dma_start(feat_sb[:], feat.rearrange("(p b) r -> p b r", b=CB))
+        nc.scalar.dma_start(w_sb[:], w.rearrange("(p b) i -> p b i", b=CB))
         nc.sync.dma_start(offsets[:], offs)
         for cb in range(CB):
-            nc.sync.dma_start(windows[cb][:], base[cb * P : (cb + 1) * P, :])
+            nc.sync.dma_start(windows[cb][:], base_blocks[:, cb, :])
 
         identity = held.tile([P, P], BF16, name="identity")
         make_identity(nc, identity[:])
@@ -93,4 +95,4 @@ def tile_diffpooling_kernel(tc, feat, w, base, offs, out):
             u_sb = held.tile([P, N], F32, name=f"u_sb{cb}")
             nc.scalar.copy(u_sb[:], u_ps[:])
             nc.vector.tensor_tensor(windows[cb][:].indirect(offsets[:]), u_sb[:], rsize[:], MULT)
-            nc.sync.dma_start(out[cb * P : (cb + 1) * P, :], windows[cb][:])
+            nc.sync.dma_start(out_blocks[:, cb, :], windows[cb][:])

@@ -75,24 +75,23 @@ def tile_diffpooling_kernel(tc, feat, w, base, offs, out):
             nc.vector.tensor_scalar(a_sb[rb][:], e_sb[rb][:], e_rsum[rb][:], None, op0=MULT)
 
         size_ps = psum.tile([P, N], F32, name="size_ps")
+        u_ps = [psum.tile([P, N], F32, name=f"u_ps{cb}") for cb in range(CB)]
         for rb in range(RB):
-            nc.tensor.matmul(
-                size_ps[:], ones[:], a_sb[rb][:], start=(rb == 0), stop=(rb == RB - 1)
-            )
+            first, last = rb == 0, rb == RB - 1
+            nc.tensor.matmul(size_ps[:], ones[:], a_sb[rb][:], start=first, stop=last)
+            for cb in range(CB):
+                nc.tensor.matmul(
+                    u_ps[cb][:],
+                    featT_sb[rb][:, cb * P : (cb + 1) * P],
+                    a_sb[rb][:],
+                    start=first,
+                    stop=last,
+                )
         rsize = held.tile([P, N], F32, name="rsize")
         nc.vector.reciprocal(rsize[:], size_ps[:])
 
         for cb in range(CB):
-            u_ps = psum.tile([P, N], F32, name=f"u_ps{cb}")
-            for rb in range(RB):
-                nc.tensor.matmul(
-                    u_ps[:],
-                    featT_sb[rb][:, cb * P : (cb + 1) * P],
-                    a_sb[rb][:],
-                    start=(rb == 0),
-                    stop=(rb == RB - 1),
-                )
             u_sb = held.tile([P, N], F32, name=f"u_sb{cb}")
-            nc.scalar.copy(u_sb[:], u_ps[:])
+            nc.scalar.copy(u_sb[:], u_ps[cb][:])
             nc.vector.tensor_tensor(windows[cb][:].indirect(offsets[:]), u_sb[:], rsize[:], MULT)
             nc.sync.dma_start(out_blocks[:, cb, :], windows[cb][:])

@@ -37,6 +37,10 @@ def tile_diffpooling_kernel(tc, feat, w, base, offs, out):
         ones = held.tile([P, P], BF16, name="ones")
         nc.gpsimd.memset(ones[:], 1.0)
 
+        scratch = held.tile([P, 1], F32, name="scratch")
+        nc.vector.memset(scratch[:], 0.0)
+        nc.scalar.activation(scratch[:], scratch[:], EXP)
+
         t_ps = [psum.tile([P, N], F32, name=f"t_ps{rb}") for rb in range(RB)]
         for rb in range(RB):
             for cb in range(CB):

@@ -34,12 +34,8 @@ def tile_diffpooling_kernel(tc, feat, w, base, offs, out):
 
         identity = held.tile([P, P], BF16, name="identity")
         make_identity(nc, identity[:])
-        ones = held.tile([P, P], BF16, name="ones")
-        nc.gpsimd.memset(ones[:], 1.0)
-
-        scratch = held.tile([P, 1], F32, name="scratch")
-        nc.vector.memset(scratch[:], 0.0)
-        nc.scalar.activation(scratch[:], scratch[:], EXP)
+        identity_f32 = held.tile([P, P], F32, name="identity_f32")
+        make_identity(nc, identity_f32[:])
 
         t_ps = [psum.tile([P, N], F32, name=f"t_ps{rb}") for rb in range(RB)]
         for rb in range(RB):
@@ -78,11 +74,11 @@ def tile_diffpooling_kernel(tc, feat, w, base, offs, out):
             nc.vector.reciprocal(e_rsum[rb][:], e_sum[rb][:])
             nc.vector.tensor_scalar(a_sb[rb][:], e_sb[rb][:], e_rsum[rb][:], None, op0=MULT)
 
-        size_ps = psum.tile([P, N], F32, name="size_ps")
+        size_ps = psum.tile([P, 1], F32, name="size_ps")
         u_ps = [psum.tile([P, N], F32, name=f"u_ps{cb}") for cb in range(CB)]
         for rb in range(RB):
             first, last = rb == 0, rb == RB - 1
-            nc.tensor.matmul(size_ps[:], ones[:], a_sb[rb][:], start=first, stop=last)
+            nc.tensor.matmul(size_ps[:], e_sb[rb][:], e_rsum[rb][:], start=first, stop=last)
             for cb in range(CB):
                 nc.tensor.matmul(
                     u_ps[cb][:],
@@ -91,8 +87,13 @@ def tile_diffpooling_kernel(tc, feat, w, base, offs, out):
                     start=first,
                     stop=last,
                 )
+        rsize_col = held.tile([P, 1], F32, name="rsize_col")
+        nc.vector.reciprocal(rsize_col[:], size_ps[:])
+
+        rsize_ps = psum.tile([P, N], F32, name="rsize_ps")
+        nc.tensor.transpose(rsize_ps[:], rsize_col[:].to_broadcast([P, P]), identity_f32[:])
         rsize = held.tile([P, N], F32, name="rsize")
-        nc.vector.reciprocal(rsize[:], size_ps[:])
+        nc.vector.tensor_copy(rsize[:], rsize_ps[:])
 
         for cb in range(CB):
             u_sb = held.tile([P, N], F32, name=f"u_sb{cb}")

@@ -36,6 +36,8 @@ def tile_diffpooling_kernel(tc, feat, w, base, offs, out):
         make_identity(nc, identity[:])
         identity_f32 = held.tile([P, P], F32, name="identity_f32")
         make_identity(nc, identity_f32[:])
+        ones_col = held.tile([P, 1], BF16, name="ones_col")
+        nc.vector.memset(ones_col[:], 1.0)
 
         t_ps = [psum.tile([P, N], F32, name=f"t_ps{rb}") for rb in range(RB)]
         for rb in range(RB):
@@ -78,7 +80,7 @@ def tile_diffpooling_kernel(tc, feat, w, base, offs, out):
         u_ps = [psum.tile([P, N], F32, name=f"u_ps{cb}") for cb in range(CB)]
         for rb in range(RB):
             first, last = rb == 0, rb == RB - 1
-            nc.tensor.matmul(size_ps[:], e_sb[rb][:], e_rsum[rb][:], start=first, stop=last)
+            nc.tensor.matmul(size_ps[:], a_sb[rb][:], ones_col[:], start=first, stop=last)
             for cb in range(CB):
                 nc.tensor.matmul(
                     u_ps[cb][:],

@@ -5,6 +5,8 @@ P = 128
 C, R, N, S = 256, 256, 128, 512
 CB = C // P
 RB = R // P
+Q = 32
+NQ = N // Q
 
 FLOPS = 2 * R * C * N + 2 * C * R * N + 2 * R * N
 
@@ -34,10 +36,8 @@ def tile_diffpooling_kernel(tc, feat, w, base, offs, out):
 
         identity = held.tile([P, P], BF16, name="identity")
         make_identity(nc, identity[:])
-        identity_f32 = held.tile([P, P], F32, name="identity_f32")
-        make_identity(nc, identity_f32[:])
-        ones_col = held.tile([P, 1], BF16, name="ones_col")
-        nc.vector.memset(ones_col[:], 1.0)
+        ones = held.tile([P, P], BF16, name="ones")
+        nc.vector.memset(ones[:], 1.0)
 
         t_ps = [psum.tile([P, N], F32, name=f"t_ps{rb}") for rb in range(RB)]
         for rb in range(RB):
@@ -50,11 +50,11 @@ def tile_diffpooling_kernel(tc, feat, w, base, offs, out):
                     stop=(cb == CB - 1),
                 )
 
-        featT_ps = [psum.tile([P, C], BF16, name=f"featT_ps{rb}") for rb in range(RB)]
+        featT_ps = psum.tile([P, RB, C], BF16, name="featT_ps", tag="featT_then_size")
         for rb in range(RB):
             for cb in range(CB):
                 nc.tensor.transpose(
-                    featT_ps[rb][:, cb * P : (cb + 1) * P],
+                    featT_ps[:, rb, cb * P : (cb + 1) * P],
                     feat_sb[:, cb, rb * P : (rb + 1) * P],
                     identity[:],
                 )
@@ -70,17 +70,17 @@ def tile_diffpooling_kernel(tc, feat, w, base, offs, out):
             nc.scalar.activation(
                 e_sb[rb][:], t_ps[rb][:], EXP, bias=neg_max[rb][:], accum_out=e_sum[rb][:]
             )
-        nc.vector.tensor_copy(featT_sb[0][:], featT_ps[0][:])
-        nc.scalar.copy(featT_sb[1][:], featT_ps[1][:])
+        for rb in range(RB):
+            nc.scalar.copy(featT_sb[rb][:], featT_ps[:, rb, :])
         for rb in range(RB):
             nc.vector.reciprocal(e_rsum[rb][:], e_sum[rb][:])
             nc.vector.tensor_scalar(a_sb[rb][:], e_sb[rb][:], e_rsum[rb][:], None, op0=MULT)
 
-        size_ps = psum.tile([P, 1], F32, name="size_ps")
+        size_ps = psum.tile([P, N], F32, name="size_ps", tag="featT_then_size")
         u_ps = [psum.tile([P, N], F32, name=f"u_ps{cb}") for cb in range(CB)]
         for rb in range(RB):
             first, last = rb == 0, rb == RB - 1
-            nc.tensor.matmul(size_ps[:], a_sb[rb][:], ones_col[:], start=first, stop=last)
+            nc.tensor.matmul(size_ps[:], ones[:], a_sb[rb][:], start=first, stop=last)
             for cb in range(CB):
                 nc.tensor.matmul(
                     u_ps[cb][:],
@@ -89,13 +89,18 @@ def tile_diffpooling_kernel(tc, feat, w, base, offs, out):
                     start=first,
                     stop=last,
                 )
-        rsize_col = held.tile([P, 1], F32, name="rsize_col")
-        nc.vector.reciprocal(rsize_col[:], size_ps[:])
 
-        rsize_ps = psum.tile([P, N], F32, name="rsize_ps")
-        nc.tensor.transpose(rsize_ps[:], rsize_col[:].to_broadcast([P, P]), identity_f32[:])
-        rsize = held.tile([P, N], F32, name="rsize")
-        nc.vector.tensor_copy(rsize[:], rsize_ps[:])
+        size_sq = held.tile([P, N], F32, name="size_sq", align_bytes=64)
+        nc.vector.transpose(size_sq[:], size_ps[:])
+        rsize_own = held.tile([P, NQ], F32, name="rsize_own")
+        nc.vector.reciprocal(rsize_own[:], size_sq[:].rearrange("p (k i) -> p k i", i=Q)[:, :, 0])
+        rsize_sq = held.tile([P, N], F32, name="rsize_sq", align_bytes=64)
+        nc.vector.tensor_copy(
+            rsize_sq[:].rearrange("p (k i) -> p k i", i=Q),
+            rsize_own[:].unsqueeze(2).to_broadcast([P, NQ, Q]),
+        )
+        rsize = held.tile([P, N], F32, name="rsize", align_bytes=64)
+        nc.vector.transpose(rsize[:], rsize_sq[:])
 
         for cb in range(CB):
             u_sb = held.tile([P, N], F32, name=f"u_sb{cb}")

@@ -5,8 +5,6 @@ P = 128
 C, R, N, S = 256, 256, 128, 512
 CB = C // P
 RB = R // P
-Q = 32
-NQ = N // Q
 
 FLOPS = 2 * R * C * N + 2 * C * R * N + 2 * R * N
 
@@ -90,17 +88,8 @@ def tile_diffpooling_kernel(tc, feat, w, base, offs, out):
                     stop=last,
                 )
 
-        size_sq = held.tile([P, N], F32, name="size_sq", align_bytes=64)
-        nc.vector.transpose(size_sq[:], size_ps[:])
-        rsize_own = held.tile([P, NQ], F32, name="rsize_own")
-        nc.vector.reciprocal(rsize_own[:], size_sq[:].rearrange("p (k i) -> p k i", i=Q)[:, :, 0])
-        rsize_sq = held.tile([P, N], F32, name="rsize_sq", align_bytes=64)
-        nc.vector.tensor_copy(
-            rsize_sq[:].rearrange("p (k i) -> p k i", i=Q),
-            rsize_own[:].unsqueeze(2).to_broadcast([P, NQ, Q]),
-        )
-        rsize = held.tile([P, N], F32, name="rsize", align_bytes=64)
-        nc.vector.transpose(rsize[:], rsize_sq[:])
+        rsize = held.tile([P, N], F32, name="rsize")
+        nc.vector.reciprocal(rsize[:], size_ps[:])
 
         for cb in range(CB):
             u_sb = held.tile([P, N], F32, name=f"u_sb{cb}")

@@ -75,17 +75,20 @@ def tile_diffpooling_kernel(tc, feat, w, base, offs, out):
             nc.vector.tensor_scalar(a_sb[rb][:], e_sb[rb][:], e_rsum[rb][:], None, op0=MULT)
 
         size_ps = psum.tile([P, N], F32, name="size_ps", tag="featT_then_size")
-        u_ps = [psum.tile([P, N], F32, name=f"u_ps{cb}") for cb in range(CB)]
         for rb in range(RB):
-            first, last = rb == 0, rb == RB - 1
-            nc.tensor.matmul(size_ps[:], ones[:], a_sb[rb][:], start=first, stop=last)
-            for cb in range(CB):
+            nc.tensor.matmul(
+                size_ps[:], ones[:], a_sb[rb][:], start=(rb == 0), stop=(rb == RB - 1)
+            )
+
+        u_ps = [psum.tile([P, N], F32, name=f"u_ps{cb}") for cb in range(CB)]
+        for cb in range(CB):
+            for rb in reversed(range(RB)):
                 nc.tensor.matmul(
                     u_ps[cb][:],
                     featT_sb[rb][:, cb * P : (cb + 1) * P],
                     a_sb[rb][:],
-                    start=first,
-                    stop=last,
+                    start=(rb == RB - 1),
+                    stop=(rb == 0),
                 )
 
         rsize = held.tile([P, N], F32, name="rsize")

@@ -80,11 +80,11 @@ def tile_diffpooling_kernel(tc, feat, w, base, offs, out):
                 size_ps[:], ones[:], a_sb[rb][:], start=(rb == 0), stop=(rb == RB - 1)
             )
 
-        u_ps = [psum.tile([P, N], F32, name=f"u_ps{cb}") for cb in range(CB)]
+        u_ps = psum.tile([P, CB, N], F32, name="u_ps")
         for cb in range(CB):
             for rb in reversed(range(RB)):
                 nc.tensor.matmul(
-                    u_ps[cb][:],
+                    u_ps[:, cb, :],
                     featT_sb[rb][:, cb * P : (cb + 1) * P],
                     a_sb[rb][:],
                     start=(rb == RB - 1),
@@ -94,8 +94,10 @@ def tile_diffpooling_kernel(tc, feat, w, base, offs, out):
         rsize = held.tile([P, N], F32, name="rsize")
         nc.vector.reciprocal(rsize[:], size_ps[:])
 
+        u_sb = held.tile([P, CB, N], F32, name="u_sb")
+        nc.scalar.copy(u_sb[:], u_ps[:])
         for cb in range(CB):
-            u_sb = held.tile([P, N], F32, name=f"u_sb{cb}")
-            nc.scalar.copy(u_sb[:], u_ps[cb][:])
-            nc.vector.tensor_tensor(windows[cb][:].indirect(offsets[:]), u_sb[:], rsize[:], MULT)
+            nc.vector.tensor_tensor(
+                windows[cb][:].indirect(offsets[:]), u_sb[:, cb, :], rsize[:], MULT
+            )
             nc.sync.dma_start(out_blocks[:, cb, :], windows[cb][:])

@@ -32,10 +32,8 @@ def tile_diffpooling_kernel(tc, feat, w, base, offs, out):
         for cb in range(CB):
             nc.sync.dma_start(windows[cb][:], base_blocks[:, cb, :])
 
-        identity = held.tile([P, P], BF16, name="identity")
+        identity = held.tile([P, P], BF16, name="identity", tag="identity_then_ones")
         make_identity(nc, identity[:])
-        ones = held.tile([P, P], BF16, name="ones")
-        nc.vector.memset(ones[:], 1.0)
 
         t_ps = [psum.tile([P, N], F32, name=f"t_ps{rb}") for rb in range(RB)]
         for rb in range(RB):
@@ -48,7 +46,7 @@ def tile_diffpooling_kernel(tc, feat, w, base, offs, out):
                     stop=(cb == CB - 1),
                 )
 
-        featT_ps = psum.tile([P, RB, C], BF16, name="featT_ps", tag="featT_then_size")
+        featT_ps = psum.tile([P, RB, C], BF16, name="featT_ps")
         for rb in range(RB):
             for cb in range(CB):
                 nc.tensor.transpose(
@@ -57,6 +55,9 @@ def tile_diffpooling_kernel(tc, feat, w, base, offs, out):
                     identity[:],
                 )
         featT_sb = [held.tile([P, C], BF16, name=f"featT_sb{rb}") for rb in range(RB)]
+
+        ones = held.tile([P, P], BF16, name="ones", tag="identity_then_ones")
+        nc.gpsimd.memset(ones[:], 1.0)
 
         neg_max = [held.tile([P, 1], F32, name=f"neg_max{rb}") for rb in range(RB)]
         e_sb = [held.tile([P, N], F32, name=f"e_sb{rb}") for rb in range(RB)]
@@ -74,7 +75,7 @@ def tile_diffpooling_kernel(tc, feat, w, base, offs, out):
             nc.vector.reciprocal(e_rsum[rb][:], e_sum[rb][:])
             nc.vector.tensor_scalar(a_sb[rb][:], e_sb[rb][:], e_rsum[rb][:], None, op0=MULT)
 
-        size_ps = psum.tile([P, N], F32, name="size_ps", tag="featT_then_size")
+        size_ps = psum.tile([P, N], F32, name="size_ps")
         for rb in range(RB):
             nc.tensor.matmul(
                 size_ps[:], ones[:], a_sb[rb][:], start=(rb == 0), stop=(rb == RB - 1)

@@ -81,24 +81,24 @@ def tile_diffpooling_kernel(tc, feat, w, base, offs, out):
                 size_ps[:], ones[:], a_sb[rb][:], start=(rb == 0), stop=(rb == RB - 1)
             )
 
-        u_ps = psum.tile([P, CB, N], F32, name="u_ps")
-        for cb in range(CB):
-            for rb in reversed(range(RB)):
+        u_ps = [psum.tile([P, N], F32, name=f"u_ps{cb}") for cb in range(CB)]
+        for rb in range(RB):
+            for cb in range(CB):
                 nc.tensor.matmul(
-                    u_ps[:, cb, :],
+                    u_ps[cb][:],
                     featT_sb[rb][:, cb * P : (cb + 1) * P],
                     a_sb[rb][:],
-                    start=(rb == RB - 1),
-                    stop=(rb == 0),
+                    start=(rb == 0),
+                    stop=(rb == RB - 1),
                 )
 
         rsize = held.tile([P, N], F32, name="rsize")
         nc.vector.reciprocal(rsize[:], size_ps[:])
 
-        u_sb = held.tile([P, CB, N], F32, name="u_sb")
-        nc.scalar.copy(u_sb[:], u_ps[:])
+        u_sb = [held.tile([P, N], F32, name=f"u_sb{cb}") for cb in range(CB)]
         for cb in range(CB):
+            nc.scalar.copy(u_sb[cb][:], u_ps[cb][:])
             nc.vector.tensor_tensor(
-                windows[cb][:].indirect(offsets[:]), u_sb[:, cb, :], rsize[:], MULT
+                windows[cb][:].indirect(offsets[:]), u_sb[cb][:], rsize[:], MULT
             )
             nc.sync.dma_start(out_blocks[:, cb, :], windows[cb][:])

@@ -92,13 +92,20 @@ def tile_diffpooling_kernel(tc, feat, w, base, offs, out):
                     stop=(rb == RB - 1),
                 )
 
+        H = N // 2
         rsize = held.tile([P, N], F32, name="rsize")
-        nc.vector.reciprocal(rsize[:], size_ps[:])
+        halves = [slice(h * H, (h + 1) * H) for h in range(2)]
+        for half in halves:
+            nc.vector.reciprocal(rsize[:, half], size_ps[:, half])
 
         u_sb = [held.tile([P, N], F32, name=f"u_sb{cb}") for cb in range(CB)]
         for cb in range(CB):
             nc.scalar.copy(u_sb[cb][:], u_ps[cb][:])
-            nc.vector.tensor_tensor(
-                windows[cb][:].indirect(offsets[:]), u_sb[cb][:], rsize[:], MULT
-            )
+            for part in halves if cb == 0 else [slice(0, N)]:
+                nc.vector.tensor_tensor(
+                    windows[cb][:].indirect(offsets[:, part.start // 16 : part.stop // 16]),
+                    u_sb[cb][:, part],
+                    rsize[:, part],
+                    MULT,
+                )
             nc.sync.dma_start(out_blocks[:, cb, :], windows[cb][:])

@@ -49,10 +49,12 @@ def tile_diffpooling_kernel(tc, feat, w, base, offs, out):
         featT_ps = psum.tile([P, RB, C], BF16, name="featT_ps")
         for rb in range(RB):
             for cb in range(CB):
-                nc.tensor.transpose(
+                nc.tensor.matmul(
                     featT_ps[:, rb, cb * P : (cb + 1) * P],
                     feat_sb[:, cb, rb * P : (rb + 1) * P],
                     identity[:],
+                    start=True,
+                    stop=True,
                 )
         featT_sb = [held.tile([P, C], BF16, name=f"featT_sb{rb}") for rb in range(RB)]
 

import concourse.mybir as mybir
from concourse.masks import make_identity

P = 128
C, R, N, S = 256, 256, 128, 512
CB = C // P
RB = R // P

FLOPS = 2 * R * C * N + 2 * C * R * N + 2 * R * N

BF16, F32, U16 = mybir.dt.bfloat16, mybir.dt.float32, mybir.dt.uint16
EXP = mybir.ActivationFunctionType.Exp
MULT, MAX = mybir.AluOpType.mult, mybir.AluOpType.max
X = mybir.AxisListType.X


def tile_diffpooling_kernel(tc, feat, w, base, offs, out):
    nc = tc.nc
    with (
        tc.tile_pool(name="held", bufs=1) as held,
        tc.psum_pool(name="psum", bufs=1) as psum,
    ):
        feat_sb = held.tile([P, CB, R], BF16, name="feat_sb")
        w_sb = held.tile([P, CB, N], BF16, name="w_sb")
        base_blocks = base.rearrange("(p b) s -> p b s", b=CB)
        out_blocks = out.rearrange("(p b) s -> p b s", b=CB)
        offsets = held.tile([P, N // 16], U16, name="offsets")
        windows = [held.tile([P, S], F32, name=f"window{cb}") for cb in range(CB)]
        nc.sync.dma_start(feat_sb[:], feat.rearrange("(p b) r -> p b r", b=CB))
        nc.scalar.dma_start(w_sb[:], w.rearrange("(p b) i -> p b i", b=CB))
        nc.sync.dma_start(offsets[:], offs)
        for cb in range(CB):
            nc.sync.dma_start(windows[cb][:], base_blocks[:, cb, :])

        identity = held.tile([P, P], BF16, name="identity", tag="identity_then_ones")
        make_identity(nc, identity[:])

        t_ps = [psum.tile([P, N], F32, name=f"t_ps{rb}") for rb in range(RB)]
        for rb in range(RB):
            for cb in range(CB):
                nc.tensor.matmul(
                    t_ps[rb][:],
                    feat_sb[:, cb, rb * P : (rb + 1) * P],
                    w_sb[:, cb, :],
                    start=(cb == 0),
                    stop=(cb == CB - 1),
                )

        featT_ps = psum.tile([P, RB, C], BF16, name="featT_ps")
        for rb in range(RB):
            for cb in range(CB):
                nc.tensor.matmul(
                    featT_ps[:, rb, cb * P : (cb + 1) * P],
                    feat_sb[:, cb, rb * P : (rb + 1) * P],
                    identity[:],
                    start=True,
                    stop=True,
                )
        featT_sb = [held.tile([P, C], BF16, name=f"featT_sb{rb}") for rb in range(RB)]

        ones = held.tile([P, P], BF16, name="ones", tag="identity_then_ones")
        nc.gpsimd.memset(ones[:], 1.0)

        neg_max = [held.tile([P, 1], F32, name=f"neg_max{rb}") for rb in range(RB)]
        e_sb = [held.tile([P, N], F32, name=f"e_sb{rb}") for rb in range(RB)]
        e_sum = [held.tile([P, 1], F32, name=f"e_sum{rb}") for rb in range(RB)]
        e_rsum = [held.tile([P, 1], F32, name=f"e_rsum{rb}") for rb in range(RB)]
        a_sb = [held.tile([P, N], BF16, name=f"a_sb{rb}") for rb in range(RB)]
        for rb in range(RB):
            nc.vector.tensor_reduce(neg_max[rb][:], t_ps[rb][:], axis=X, op=MAX, negate=True)
            nc.scalar.activation(
                e_sb[rb][:], t_ps[rb][:], EXP, bias=neg_max[rb][:], accum_out=e_sum[rb][:]
            )
        for rb in range(RB):
            nc.scalar.copy(featT_sb[rb][:], featT_ps[:, rb, :])
        for rb in range(RB):
            nc.vector.reciprocal(e_rsum[rb][:], e_sum[rb][:])
            nc.vector.tensor_scalar(a_sb[rb][:], e_sb[rb][:], e_rsum[rb][:], None, op0=MULT)

        size_ps = psum.tile([P, N], F32, name="size_ps")
        for rb in range(RB):
            nc.tensor.matmul(
                size_ps[:], ones[:], a_sb[rb][:], start=(rb == 0), stop=(rb == RB - 1)
            )

        u_ps = [psum.tile([P, N], F32, name=f"u_ps{cb}") for cb in range(CB)]
        for rb in range(RB):
            for cb in range(CB):
                nc.tensor.matmul(
                    u_ps[cb][:],
                    featT_sb[rb][:, cb * P : (cb + 1) * P],
                    a_sb[rb][:],
                    start=(rb == 0),
                    stop=(rb == RB - 1),
                )

        H = N // 2
        rsize = held.tile([P, N], F32, name="rsize")
        halves = [slice(h * H, (h + 1) * H) for h in range(2)]
        for half in halves:
            nc.vector.reciprocal(rsize[:, half], size_ps[:, half])

        u_sb = [held.tile([P, N], F32, name=f"u_sb{cb}") for cb in range(CB)]
        for cb in range(CB):
            nc.scalar.copy(u_sb[cb][:], u_ps[cb][:])
            for part in halves if cb == 0 else [slice(0, N)]:
                nc.vector.tensor_tensor(
                    windows[cb][:].indirect(offsets[:, part.start // 16 : part.stop // 16]),
                    u_sb[cb][:, part],
                    rsize[:, part],
                    MULT,
                )
            nc.sync.dma_start(out_blocks[:, cb, :], windows[cb][:])
